import numpy as np
import ml_dtypes

BF16 = ml_dtypes.bfloat16


def bf(x):
    return np.asarray(x, np.float32).astype(BF16)


def f32(x):
    return np.asarray(x, np.float32)


def f64(x):
    return np.asarray(x).astype(np.float64)


def striped(idx):
    return np.tile(idx.reshape(-1, 16).T, (8, 1))


P, S, T, F, K, R, N = 128, 1024, 8, 128, 3, 2, 1024


def tree_sums(picked, w):
    return (picked[:, None, :] * f64(w)[None, :, :]).reshape(P, -1, T, F).sum(axis=-1)


def softmax_mid(v):
    e = np.exp(v - v.max(axis=1, keepdims=True))
    return e / e.sum(axis=1, keepdims=True)


def setup_inputs():
    return {"d": bf(np.random.standard_normal((P, S))), "w_gate": bf(np.random.standard_normal((R, N)) / np.sqrt(F)), "b_gate": f32(0.5 * np.random.standard_normal((R, T))), "w_cls": bf(np.random.standard_normal((K, N)) / np.sqrt(F)), "b_cls": f32(0.5 * np.random.standard_normal((K, T))), "offs": striped(np.random.permutation(np.tile(np.arange(S), 2))[:N])}


def reference(d, w_gate, b_gate, w_cls, b_cls, offs):
    idx = offs[:16].T.reshape(-1)
    picked = f64(d)[:, idx]
    u = tree_sums(picked, w_gate) + f64(b_gate)[None, :, :]
    v = tree_sums(picked, w_cls) + f64(b_cls)[None, :, :]
    gate = softmax_mid(u)[:, R - 1, :]
    p = softmax_mid(v)
    return (p * gate[:, None, :]).sum(axis=-1) / gate.sum(axis=-1, keepdims=True)

@@ -1,0 +1,139 @@
+import concourse.mybir as mybir
+from concourse.masks import make_identity
+
+F32 = mybir.dt.float32
+BF16 = mybir.dt.bfloat16
+U16 = mybir.dt.uint16
+ALU = mybir.AluOpType
+ACT = mybir.ActivationFunctionType
+AX = mybir.AxisListType
+
+P = 128
+S = 1024
+N = 1024
+T = 8
+F = N // T
+K = 3
+ROWS = 5
+DIFFS = ((1, 0), (3, 2), (4, 2))
+BANK = 512
+LANES = 8
+
+FLOPS = 2 * P * N * ROWS
+
+
+def tile_forestclf_kernel(tc, d, w_gate, b_gate, w_cls, b_cls, offs, out):
+    nc = tc.nc
+    with (
+        tc.tile_pool(name="held", bufs=1) as held,
+        tc.psum_pool(name="spread", bufs=6) as spread,
+        tc.psum_pool(name="pack", bufs=1) as pack,
+    ):
+        offsets = held.tile([P, N // 16], U16, name="offsets")
+        nc.sync.dma_start(offsets[:], offs)
+        w_rows = held.tile([ROWS, N], BF16)
+        nc.scalar.dma_start(w_rows[0:2, :], w_gate)
+        nc.scalar.dma_start(w_rows[2:5, :], w_cls)
+        d_bf = held.tile([P, S], BF16)
+        nc.sync.dma_start(d_bf[:], d)
+        b_rows = held.tile([P, ROWS, T], F32)
+        nc.gpsimd.dma_start(
+            b_rows[:, 0:2, :].rearrange("p r t -> p (r t)"), b_gate.rearrange("r t -> (r t)").partition_broadcast(P)
+        )
+        nc.gpsimd.dma_start(
+            b_rows[:, 2:5, :].rearrange("p r t -> p (r t)"), b_cls.rearrange("r t -> (r t)").partition_broadcast(P)
+        )
+
+        eye = held.tile([P, P], F32)
+        make_identity(nc, eye[:])
+        signs = held.tile([ROWS, K, P], BF16)
+        for c, (plus, minus) in enumerate(DIFFS):
+            nc.vector.tensor_sub(
+                signs[:, c, :],
+                eye[0:ROWS, plus : plus + 1].to_broadcast([ROWS, P]),
+                eye[0:ROWS, minus : minus + 1].to_broadcast([ROWS, P]),
+            )
+        of_group = held.tile([P, P // LANES], F32)
+        nc.vector.tensor_reduce(of_group[:], eye[:].rearrange("p (q s) -> p q s", s=LANES), axis=AX.X, op=ALU.add)
+        of_lane = held.tile([P, LANES], F32)
+        nc.vector.tensor_reduce(of_lane[:], eye[:].rearrange("p (q s) -> p s q", s=LANES), axis=AX.X, op=ALU.add)
+
+        w_diff = held.tile([P, K, N], F32)
+        for c in range(K):
+            for h in range(N // BANK):
+                bank = spread.tile([P, BANK], F32)
+                nc.tensor.matmul(bank[:], signs[:, c, :], w_rows[:, h * BANK : (h + 1) * BANK], start=True, stop=True)
+                nc.scalar.copy(w_diff[:, c, h * BANK : (h + 1) * BANK], bank[:])
+
+        table = held.tile([P, S], F32)
+        nc.vector.tensor_copy(table[:], d_bf[:])
+
+        b_diff = held.tile([P, K, T], F32)
+        nc.gpsimd.tensor_sub(b_diff[:, 0, :], b_rows[:, 1, :], b_rows[:, 0, :])
+        nc.gpsimd.tensor_sub(b_diff[:, 1:3, :], b_rows[:, 3:5, :], b_rows[:, 2:3, :].to_broadcast([P, 2, T]))
+
+        score = held.tile([P, 1 + K, T], F32)
+        nc.gpsimd.memset(score[:, 1, :], 0.0)
+
+        prod = held.tile([P, K, N], F32)
+        tree_sum = held.tile([P, K, T], F32)
+
+        def walk_list(c):
+            nc.vector.tensor_tensor(prod[:, c, :], table[:].indirect(offsets[:]), w_diff[:, c, :], ALU.mult)
+            nc.vector.tensor_reduce(
+                tree_sum[:, c, :], prod[:, c, :].rearrange("p (t f) -> p t f", f=F), axis=AX.X, op=ALU.add
+            )
+
+        walk_list(0)
+        x = score[:, 0, :]
+        nc.vector.tensor_add(x, tree_sum[:, 0, :], b_diff[:, 0, :])
+        gate_arg = held.tile([P, 2, T], F32)
+        nc.vector.tensor_scalar_min(gate_arg[:, 0, :], x, 0.0)
+        nc.vector.tensor_scalar(gate_arg[:, 1, :], x, -1.0, 0.0, ALU.mult, ALU.min)
+        gate_exp = held.tile([P, 2, T], F32)
+        nc.scalar.activation(gate_exp[:], gate_arg[:], ACT.Exp)
+        gate_den = held.tile([P, T], F32)
+        nc.vector.tensor_add(gate_den[:], gate_exp[:, 0, :], gate_exp[:, 1, :])
+        gate_rec = held.tile([P, T], F32)
+        nc.vector.reciprocal(gate_rec[:], gate_den[:])
+        gate = held.tile([P, T], F32)
+        nc.vector.tensor_mul(gate[:], gate_exp[:, 0, :], gate_rec[:])
+        gate_sum = held.tile([P, 1], F32)
+        nc.vector.tensor_reduce(gate_sum[:], gate[:], axis=AX.X, op=ALU.add)
+        gate_sum_rec = held.tile([P, 1], F32)
+        nc.vector.reciprocal(gate_sum_rec[:], gate_sum[:])
+        share = held.tile([P, T], F32)
+        nc.vector.tensor_scalar_mul(share[:], gate[:], gate_sum_rec[:])
+
+        walk_list(1)
+        walk_list(2)
+        nc.vector.tensor_add(score[:, 2:4, :], tree_sum[:, 1:3, :], b_diff[:, 1:3, :])
+        cls = score[:, 1 : 1 + K, :]
+        top = held.tile([P, T], F32)
+        nc.vector.tensor_reduce(top[:], cls.rearrange("p k t -> p t k"), axis=AX.X, op=ALU.max)
+        cls_arg = held.tile([P, K, T], F32)
+        nc.vector.tensor_sub(cls_arg[:], cls, top[:].unsqueeze(1).to_broadcast([P, K, T]))
+        cls_exp = held.tile([P, K, T], F32)
+        nc.scalar.activation(cls_exp[:], cls_arg[:], ACT.Exp)
+        cls_den = held.tile([P, T], F32)
+        nc.vector.tensor_reduce(cls_den[:], cls_exp[:].rearrange("p k t -> p t k"), axis=AX.X, op=ALU.add)
+        shared = held.tile([P, K, T], F32)
+        nc.vector.tensor_mul(shared[:], cls_exp[:], share[:].unsqueeze(1).to_broadcast([P, K, T]))
+        cls_rec = held.tile([P, T], F32)
+        nc.vector.reciprocal(cls_rec[:], cls_den[:])
+        weighted = held.tile([P, K, T], F32)
+        nc.vector.tensor_mul(weighted[:], shared[:], cls_rec[:].unsqueeze(1).to_broadcast([P, K, T]))
+        mean = held.tile([P, K], F32)
+        nc.vector.tensor_reduce(mean[:], weighted[:], axis=AX.X, op=ALU.add)
+
+        blocks = held.tile([P, LANES, K], F32)
+        nc.vector.tensor_mul(
+            blocks[:],
+            of_lane[:].unsqueeze(2).to_broadcast([P, LANES, K]),
+            mean[:].unsqueeze(1).to_broadcast([P, LANES, K]),
+        )
+        packed_ps = pack.tile([P // LANES, LANES * K], F32)
+        nc.tensor.matmul(packed_ps[:], of_group[:], blocks[:].rearrange("p s k -> p (s k)"), start=True, stop=True)
+        packed = held.tile([P // LANES, LANES * K], F32)
+        nc.vector.tensor_copy(packed[:], packed_ps[:])
+        nc.sync.dma_start(out.rearrange("(q s) k -> q (s k)", s=LANES), packed[:])

@@ -16,7 +16,8 @@ F = N // T
 K = 3
 ROWS = 5
 DIFFS = ((1, 0), (3, 2), (4, 2))
-BANK = 512
+PIECE = 512
+PIECES = N // PIECE
 LANES = 8
 
 FLOPS = 2 * P * N * ROWS
@@ -26,21 +27,23 @@ def tile_forestclf_kernel(tc, d, w_gate, b_gate, w_cls, b_cls, offs, out):
     nc = tc.nc
     with (
         tc.tile_pool(name="held", bufs=1) as held,
-        tc.psum_pool(name="spread", bufs=6) as spread,
+        tc.tile_pool(name="scrap", bufs=2) as scrap,
+        tc.psum_pool(name="spread", bufs=K * PIECES) as spread,
         tc.psum_pool(name="pack", bufs=1) as pack,
     ):
-        offsets = held.tile([P, N // 16], U16, name="offsets")
-        nc.sync.dma_start(offsets[:], offs)
         w_rows = held.tile([ROWS, N], BF16)
         nc.scalar.dma_start(w_rows[0:2, :], w_gate)
         nc.scalar.dma_start(w_rows[2:5, :], w_cls)
         d_bf = held.tile([P, S], BF16)
-        nc.sync.dma_start(d_bf[:], d)
+        for h in range(2):
+            nc.sync.dma_start(d_bf[:, h * (S // 2) : (h + 1) * (S // 2)], d[:, h * (S // 2) : (h + 1) * (S // 2)])
+        offsets = held.tile([P, N // 16], U16, name="offsets")
+        nc.sync.dma_start(offsets[:], offs)
         b_rows = held.tile([P, ROWS, T], F32)
-        nc.gpsimd.dma_start(
+        nc.scalar.dma_start(
             b_rows[:, 0:2, :].rearrange("p r t -> p (r t)"), b_gate.rearrange("r t -> (r t)").partition_broadcast(P)
         )
-        nc.gpsimd.dma_start(
+        nc.scalar.dma_start(
             b_rows[:, 2:5, :].rearrange("p r t -> p (r t)"), b_cls.rearrange("r t -> (r t)").partition_broadcast(P)
         )
 
@@ -60,38 +63,64 @@ def tile_forestclf_kernel(tc, d, w_gate, b_gate, w_cls, b_cls, offs, out):
 
         w_diff = held.tile([P, K, N], F32)
         for c in range(K):
-            for h in range(N // BANK):
-                bank = spread.tile([P, BANK], F32)
-                nc.tensor.matmul(bank[:], signs[:, c, :], w_rows[:, h * BANK : (h + 1) * BANK], start=True, stop=True)
-                nc.scalar.copy(w_diff[:, c, h * BANK : (h + 1) * BANK], bank[:])
+            for h in range(PIECES):
+                bank = spread.tile([P, PIECE], F32)
+                nc.tensor.matmul(bank[:], signs[:, c, :], w_rows[:, h * PIECE : (h + 1) * PIECE], start=True, stop=True)
+                nc.scalar.copy(w_diff[:, c, h * PIECE : (h + 1) * PIECE], bank[:])
 
         table = held.tile([P, S], F32)
-        nc.vector.tensor_copy(table[:], d_bf[:])
-
-        b_diff = held.tile([P, K, T], F32)
-        nc.gpsimd.tensor_sub(b_diff[:, 0, :], b_rows[:, 1, :], b_rows[:, 0, :])
-        nc.gpsimd.tensor_sub(b_diff[:, 1:3, :], b_rows[:, 3:5, :], b_rows[:, 2:3, :].to_broadcast([P, 2, T]))
+        for h in range(2):
+            nc.vector.tensor_copy(table[:, h * (S // 2) : (h + 1) * (S // 2)], d_bf[:, h * (S // 2) : (h + 1) * (S // 2)])
 
         score = held.tile([P, 1 + K, T], F32)
-        nc.gpsimd.memset(score[:, 1, :], 0.0)
+        score_row = (0, 2, 3)
+        nc.gpsimd.tensor_sub(score[:, 1, :], b_rows[:, 2, :], b_rows[:, 4, :])
+        b_diff = held.tile([P, K - 1, T], F32)
+        nc.gpsimd.tensor_sub(b_diff[:, 0, :], b_rows[:, 1, :], b_rows[:, 0, :])
+        nc.gpsimd.tensor_sub(b_diff[:, 1, :], b_rows[:, 3, :], b_rows[:, 4, :])
+        b_part = held.tile([P, K - 1, T], F32)
+        nc.gpsimd.tensor_scalar_mul(b_part[:], b_diff[:], 1.0 / F)
 
         prod = held.tile([P, K, N], F32)
-        tree_sum = held.tile([P, K, T], F32)
+        for c in range(K):
+            for h in range(PIECES):
+                nc.vector.tensor_tensor(
+                    prod[:, c, h * PIECE : (h + 1) * PIECE],
+                    table[:].indirect(offsets[:, h * (PIECE // 16) : (h + 1) * (PIECE // 16)]),
+                    w_diff[:, c, h * PIECE : (h + 1) * PIECE],
+                    ALU.mult,
+                )
+            if c < K - 1:
+                for t in range(T):
+                    unused = scrap.tile([P, F], F32)
+                    nc.scalar.activation(
+                        unused[:],
+                        prod[:, c, t * F : (t + 1) * F],
+                        ACT.Identity,
+                        bias=b_part[:, c, t : t + 1],
+                        accum_out=score[:, score_row[c], t : t + 1],
+                    )
+        nc.vector.tensor_reduce(
+            score[:, score_row[K - 1], :],
+            prod[:, K - 1, :].rearrange("p (t f) -> p t f", f=F),
+            axis=AX.X,
+            op=ALU.add,
+        )
 
-        def walk_list(c):
-            nc.vector.tensor_tensor(prod[:, c, :], table[:].indirect(offsets[:]), w_diff[:, c, :], ALU.mult)
-            nc.vector.tensor_reduce(
-                tree_sum[:, c, :], prod[:, c, :].rearrange("p (t f) -> p t f", f=F), axis=AX.X, op=ALU.add
-            )
-
-        walk_list(0)
         x = score[:, 0, :]
-        nc.vector.tensor_add(x, tree_sum[:, 0, :], b_diff[:, 0, :])
         gate_arg = held.tile([P, 2, T], F32)
-        nc.vector.tensor_scalar_min(gate_arg[:, 0, :], x, 0.0)
-        nc.vector.tensor_scalar(gate_arg[:, 1, :], x, -1.0, 0.0, ALU.mult, ALU.min)
+        nc.scalar.activation(gate_arg[:, 0, :], x, ACT.Relu, scale=-1.0)
+        nc.scalar.activation(gate_arg[:, 1, :], x, ACT.Relu)
         gate_exp = held.tile([P, 2, T], F32)
-        nc.scalar.activation(gate_exp[:], gate_arg[:], ACT.Exp)
+        nc.scalar.activation(gate_exp[:], gate_arg[:], ACT.Exp, scale=-1.0)
+        cls = score[:, 1 : 1 + K, :]
+        top = held.tile([P, T], F32)
+        nc.vector.tensor_reduce(top[:], cls.rearrange("p k t -> p t k"), axis=AX.X, op=ALU.max)
+        cls_arg = held.tile([P, K, T], F32)
+        nc.vector.tensor_sub(cls_arg[:], cls, top[:].unsqueeze(1).to_broadcast([P, K, T]))
+        cls_exp = held.tile([P, K, T], F32)
+        nc.scalar.activation(cls_exp[:], cls_arg[:], ACT.Exp)
+
         gate_den = held.tile([P, T], F32)
         nc.vector.tensor_add(gate_den[:], gate_exp[:, 0, :], gate_exp[:, 1, :])
         gate_rec = held.tile([P, T], F32)
@@ -102,35 +131,25 @@ def tile_forestclf_kernel(tc, d, w_gate, b_gate, w_cls, b_cls, offs, out):
         nc.vector.tensor_reduce(gate_sum[:], gate[:], axis=AX.X, op=ALU.add)
         gate_sum_rec = held.tile([P, 1], F32)
         nc.vector.reciprocal(gate_sum_rec[:], gate_sum[:])
-        share = held.tile([P, T], F32)
-        nc.vector.tensor_scalar_mul(share[:], gate[:], gate_sum_rec[:])
+        lane_share = held.tile([P, LANES], F32)
+        nc.vector.tensor_scalar_mul(lane_share[:], of_lane[:], gate_sum_rec[:])
 
-        walk_list(1)
-        walk_list(2)
-        nc.vector.tensor_add(score[:, 2:4, :], tree_sum[:, 1:3, :], b_diff[:, 1:3, :])
-        cls = score[:, 1 : 1 + K, :]
-        top = held.tile([P, T], F32)
-        nc.vector.tensor_reduce(top[:], cls.rearrange("p k t -> p t k"), axis=AX.X, op=ALU.max)
-        cls_arg = held.tile([P, K, T], F32)
-        nc.vector.tensor_sub(cls_arg[:], cls, top[:].unsqueeze(1).to_broadcast([P, K, T]))
-        cls_exp = held.tile([P, K, T], F32)
-        nc.scalar.activation(cls_exp[:], cls_arg[:], ACT.Exp)
         cls_den = held.tile([P, T], F32)
         nc.vector.tensor_reduce(cls_den[:], cls_exp[:].rearrange("p k t -> p t k"), axis=AX.X, op=ALU.add)
-        shared = held.tile([P, K, T], F32)
-        nc.vector.tensor_mul(shared[:], cls_exp[:], share[:].unsqueeze(1).to_broadcast([P, K, T]))
+        gated = held.tile([P, K, T], F32)
+        nc.vector.tensor_mul(gated[:], cls_exp[:], gate[:].unsqueeze(1).to_broadcast([P, K, T]))
         cls_rec = held.tile([P, T], F32)
         nc.vector.reciprocal(cls_rec[:], cls_den[:])
         weighted = held.tile([P, K, T], F32)
-        nc.vector.tensor_mul(weighted[:], shared[:], cls_rec[:].unsqueeze(1).to_broadcast([P, K, T]))
-        mean = held.tile([P, K], F32)
-        nc.vector.tensor_reduce(mean[:], weighted[:], axis=AX.X, op=ALU.add)
+        nc.vector.tensor_mul(weighted[:], gated[:], cls_rec[:].unsqueeze(1).to_broadcast([P, K, T]))
+        total = held.tile([P, K], F32)
+        nc.vector.tensor_reduce(total[:], weighted[:], axis=AX.X, op=ALU.add)
 
         blocks = held.tile([P, LANES, K], F32)
         nc.vector.tensor_mul(
             blocks[:],
-            of_lane[:].unsqueeze(2).to_broadcast([P, LANES, K]),
-            mean[:].unsqueeze(1).to_broadcast([P, LANES, K]),
+            lane_share[:].unsqueeze(2).to_broadcast([P, LANES, K]),
+            total[:].unsqueeze(1).to_broadcast([P, LANES, K]),
         )
         packed_ps = pack.tile([P // LANES, LANES * K], F32)
         nc.tensor.matmul(packed_ps[:], of_group[:], blocks[:].rearrange("p s k -> p (s k)"), start=True, stop=True)

@@ -10,6 +10,7 @@ AX = mybir.AxisListType
 
 P = 128
 S = 1024
+HALF = S // 2
 N = 1024
 T = 8
 F = N // T
@@ -32,14 +33,14 @@ def tile_forestclf_kernel(tc, d, w_gate, b_gate, w_cls, b_cls, offs, out):
         tc.psum_pool(name="pack", bufs=1) as pack,
     ):
         w_rows = held.tile([ROWS, N], BF16)
-        nc.scalar.dma_start(w_rows[0:2, :], w_gate)
-        nc.scalar.dma_start(w_rows[2:5, :], w_cls)
         d_bf = held.tile([P, S], BF16)
-        for h in range(2):
-            nc.sync.dma_start(d_bf[:, h * (S // 2) : (h + 1) * (S // 2)], d[:, h * (S // 2) : (h + 1) * (S // 2)])
         offsets = held.tile([P, N // 16], U16, name="offsets")
-        nc.sync.dma_start(offsets[:], offs)
         b_rows = held.tile([P, ROWS, T], F32)
+        nc.sync.dma_start(w_rows[0:2, :], w_gate)
+        nc.scalar.dma_start(w_rows[2:5, :], w_cls)
+        nc.sync.dma_start(d_bf[:, 0:HALF], d[:, 0:HALF])
+        nc.scalar.dma_start(d_bf[:, HALF:S], d[:, HALF:S])
+        nc.sync.dma_start(offsets[:], offs)
         nc.scalar.dma_start(
             b_rows[:, 0:2, :].rearrange("p r t -> p (r t)"), b_gate.rearrange("r t -> (r t)").partition_broadcast(P)
         )
@@ -69,8 +70,8 @@ def tile_forestclf_kernel(tc, d, w_gate, b_gate, w_cls, b_cls, offs, out):
                 nc.scalar.copy(w_diff[:, c, h * PIECE : (h + 1) * PIECE], bank[:])
 
         table = held.tile([P, S], F32)
-        for h in range(2):
-            nc.vector.tensor_copy(table[:, h * (S // 2) : (h + 1) * (S // 2)], d_bf[:, h * (S // 2) : (h + 1) * (S // 2)])
+        nc.vector.tensor_copy(table[:, 0:HALF], d_bf[:, 0:HALF])
+        nc.vector.tensor_copy(table[:, HALF:S], d_bf[:, HALF:S])
 
         score = held.tile([P, 1 + K, T], F32)
         score_row = (0, 2, 3)

@@ -16,10 +16,13 @@ T = 8
 F = N // T
 K = 3
 ROWS = 5
-DIFFS = ((1, 0), (3, 2), (4, 2))
+WALKS = 3
+DIFFS = ((3, 2), (1, 0), (4, 2))
 PIECE = 512
 PIECES = N // PIECE
+TREES = PIECE // F
 LANES = 8
+CAP = 1.0e30
 
 FLOPS = 2 * P * N * ROWS
 
@@ -29,7 +32,7 @@ def tile_forestclf_kernel(tc, d, w_gate, b_gate, w_cls, b_cls, offs, out):
     with (
         tc.tile_pool(name="held", bufs=1) as held,
         tc.tile_pool(name="scrap", bufs=2) as scrap,
-        tc.psum_pool(name="spread", bufs=K * PIECES) as spread,
+        tc.psum_pool(name="spread", bufs=WALKS * PIECES) as spread,
         tc.psum_pool(name="pack", bufs=1) as pack,
     ):
         w_rows = held.tile([ROWS, N], BF16)
@@ -50,7 +53,7 @@ def tile_forestclf_kernel(tc, d, w_gate, b_gate, w_cls, b_cls, offs, out):
 
         eye = held.tile([P, P], F32)
         make_identity(nc, eye[:])
-        signs = held.tile([ROWS, K, P], BF16)
+        signs = held.tile([ROWS, WALKS, P], BF16)
         for c, (plus, minus) in enumerate(DIFFS):
             nc.vector.tensor_sub(
                 signs[:, c, :],
@@ -62,72 +65,72 @@ def tile_forestclf_kernel(tc, d, w_gate, b_gate, w_cls, b_cls, offs, out):
         of_lane = held.tile([P, LANES], F32)
         nc.vector.tensor_reduce(of_lane[:], eye[:].rearrange("p (q s) -> p s q", s=LANES), axis=AX.X, op=ALU.add)
 
-        w_diff = held.tile([P, K, N], F32)
-        for c in range(K):
+        w_diff = [[held.tile([P, PIECE], F32, name=f"w_diff_{c}_{h}") for h in range(PIECES)] for c in range(WALKS)]
+        for c in range(WALKS):
             for h in range(PIECES):
                 bank = spread.tile([P, PIECE], F32)
                 nc.tensor.matmul(bank[:], signs[:, c, :], w_rows[:, h * PIECE : (h + 1) * PIECE], start=True, stop=True)
-                nc.scalar.copy(w_diff[:, c, h * PIECE : (h + 1) * PIECE], bank[:])
+                nc.scalar.copy(w_diff[c][h][:], bank[:])
 
         table = held.tile([P, S], F32)
         nc.vector.tensor_copy(table[:, 0:HALF], d_bf[:, 0:HALF])
         nc.vector.tensor_copy(table[:, HALF:S], d_bf[:, HALF:S])
 
-        score = held.tile([P, 1 + K, T], F32)
-        score_row = (0, 2, 3)
-        nc.gpsimd.tensor_sub(score[:, 1, :], b_rows[:, 2, :], b_rows[:, 4, :])
-        b_diff = held.tile([P, K - 1, T], F32)
-        nc.gpsimd.tensor_sub(b_diff[:, 0, :], b_rows[:, 1, :], b_rows[:, 0, :])
-        nc.gpsimd.tensor_sub(b_diff[:, 1, :], b_rows[:, 3, :], b_rows[:, 4, :])
-        b_part = held.tile([P, K - 1, T], F32)
+        b_diff = held.tile([P, WALKS, T], F32)
+        for c, (plus, minus) in enumerate(DIFFS):
+            nc.gpsimd.tensor_sub(b_diff[:, c, :], b_rows[:, plus, :], b_rows[:, minus, :])
+        b_part = held.tile([P, WALKS, T], F32)
         nc.gpsimd.tensor_scalar_mul(b_part[:], b_diff[:], 1.0 / F)
 
-        prod = held.tile([P, K, N], F32)
-        for c in range(K):
+        score = held.tile([P, WALKS, T], F32)
+
+        def walk_list(c, part):
             for h in range(PIECES):
+                prod = held.tile([P, PIECE], F32, name=f"prod_{c}_{h}")
                 nc.vector.tensor_tensor(
-                    prod[:, c, h * PIECE : (h + 1) * PIECE],
+                    prod[:],
                     table[:].indirect(offsets[:, h * (PIECE // 16) : (h + 1) * (PIECE // 16)]),
-                    w_diff[:, c, h * PIECE : (h + 1) * PIECE],
+                    w_diff[c][h][:],
                     ALU.mult,
                 )
-            if c < K - 1:
-                for t in range(T):
+                for t in range(h * TREES, (h + 1) * TREES):
                     unused = scrap.tile([P, F], F32)
                     nc.scalar.activation(
                         unused[:],
-                        prod[:, c, t * F : (t + 1) * F],
+                        prod[:, (t - h * TREES) * F : (t - h * TREES + 1) * F],
                         ACT.Identity,
-                        bias=b_part[:, c, t : t + 1],
-                        accum_out=score[:, score_row[c], t : t + 1],
+                        bias=part[:, t : t + 1],
+                        accum_out=score[:, c, t : t + 1],
                     )
-        nc.vector.tensor_reduce(
-            score[:, score_row[K - 1], :],
-            prod[:, K - 1, :].rearrange("p (t f) -> p t f", f=F),
-            axis=AX.X,
-            op=ALU.add,
-        )
 
-        x = score[:, 0, :]
-        gate_arg = held.tile([P, 2, T], F32)
-        nc.scalar.activation(gate_arg[:, 0, :], x, ACT.Relu, scale=-1.0)
-        nc.scalar.activation(gate_arg[:, 1, :], x, ACT.Relu)
-        gate_exp = held.tile([P, 2, T], F32)
-        nc.scalar.activation(gate_exp[:], gate_arg[:], ACT.Exp, scale=-1.0)
-        cls = score[:, 1 : 1 + K, :]
-        top = held.tile([P, T], F32)
-        nc.vector.tensor_reduce(top[:], cls.rearrange("p k t -> p t k"), axis=AX.X, op=ALU.max)
-        cls_arg = held.tile([P, K, T], F32)
-        nc.vector.tensor_sub(cls_arg[:], cls, top[:].unsqueeze(1).to_broadcast([P, K, T]))
-        cls_exp = held.tile([P, K, T], F32)
-        nc.scalar.activation(cls_exp[:], cls_arg[:], ACT.Exp)
+        def exp_of_pair(y, name):
+            arg = held.tile([P, 2, T], F32, name=f"{name}_arg")
+            nc.scalar.activation(arg[:, 0, :], y, ACT.Relu)
+            nc.scalar.activation(arg[:, 1, :], y, ACT.Relu, scale=-1.0)
+            exps = held.tile([P, 2, T], F32, name=f"{name}_exp")
+            nc.scalar.activation(exps[:], arg[:], ACT.Exp, scale=-1.0)
+            return exps
 
+        walk_list(0, b_part[:, 0, :])
+        z1 = score[:, 0, :]
+        cls_exp = exp_of_pair(z1, "cls")
+        cls_sum = held.tile([P, T], F32)
+        nc.gpsimd.tensor_add(cls_sum[:], cls_exp[:, 0, :], cls_exp[:, 1, :])
+        top_part = held.tile([P, T], F32)
+        nc.scalar.activation(top_part[:], z1, ACT.Relu, scale=1.0 / F)
+        last_part = held.tile([P, T], F32)
+        nc.gpsimd.tensor_sub(last_part[:], b_part[:, 2, :], top_part[:])
+
+        walk_list(1, b_part[:, 1, :])
+        gate_exp = exp_of_pair(score[:, 1, :], "gate")
         gate_den = held.tile([P, T], F32)
         nc.vector.tensor_add(gate_den[:], gate_exp[:, 0, :], gate_exp[:, 1, :])
         gate_rec = held.tile([P, T], F32)
         nc.vector.reciprocal(gate_rec[:], gate_den[:])
         gate = held.tile([P, T], F32)
-        nc.vector.tensor_mul(gate[:], gate_exp[:, 0, :], gate_rec[:])
+        nc.vector.tensor_mul(gate[:], gate_exp[:, 1, :], gate_rec[:])
+        gated = held.tile([P, K, T], F32)
+        nc.vector.tensor_mul(gated[:, 0:2, :], cls_exp[:], gate[:].unsqueeze(1).to_broadcast([P, 2, T]))
         gate_sum = held.tile([P, 1], F32)
         nc.vector.tensor_reduce(gate_sum[:], gate[:], axis=AX.X, op=ALU.add)
         gate_sum_rec = held.tile([P, 1], F32)
@@ -135,10 +138,12 @@ def tile_forestclf_kernel(tc, d, w_gate, b_gate, w_cls, b_cls, offs, out):
         lane_share = held.tile([P, LANES], F32)
         nc.vector.tensor_scalar_mul(lane_share[:], of_lane[:], gate_sum_rec[:])
 
+        walk_list(2, last_part[:])
+        last_exp = held.tile([P, T], F32)
+        nc.scalar.activation(last_exp[:], score[:, 2, :], ACT.Exp)
         cls_den = held.tile([P, T], F32)
-        nc.vector.tensor_reduce(cls_den[:], cls_exp[:].rearrange("p k t -> p t k"), axis=AX.X, op=ALU.add)
-        gated = held.tile([P, K, T], F32)
-        nc.vector.tensor_mul(gated[:], cls_exp[:], gate[:].unsqueeze(1).to_broadcast([P, K, T]))
+        nc.vector.scalar_tensor_tensor(cls_den[:], last_exp[:], CAP, cls_sum[:], ALU.min, ALU.add)
+        nc.vector.scalar_tensor_tensor(gated[:, 2, :], last_exp[:], CAP, gate[:], ALU.min, ALU.mult)
         cls_rec = held.tile([P, T], F32)
         nc.vector.reciprocal(cls_rec[:], cls_den[:])
         weighted = held.tile([P, K, T], F32)

@@ -40,25 +40,27 @@ def tile_forestclf_kernel(tc, d, w_gate, b_gate, w_cls, b_cls, offs, out):
         offsets = held.tile([P, N // 16], U16, name="offsets")
         b_rows = held.tile([P, ROWS, T], F32)
         nc.sync.dma_start(w_rows[0:2, :], w_gate)
-        nc.scalar.dma_start(w_rows[2:5, :], w_cls)
-        nc.sync.dma_start(d_bf[:, 0:HALF], d[:, 0:HALF])
+        nc.sync.dma_start(w_rows[2:5, :], w_cls)
         nc.scalar.dma_start(d_bf[:, HALF:S], d[:, HALF:S])
+        nc.sync.dma_start(d_bf[:, 0:HALF], d[:, 0:HALF])
         nc.sync.dma_start(offsets[:], offs)
-        nc.scalar.dma_start(
+        nc.sync.dma_start(
             b_rows[:, 0:2, :].rearrange("p r t -> p (r t)"), b_gate.rearrange("r t -> (r t)").partition_broadcast(P)
         )
-        nc.scalar.dma_start(
+        nc.sync.dma_start(
             b_rows[:, 2:5, :].rearrange("p r t -> p (r t)"), b_cls.rearrange("r t -> (r t)").partition_broadcast(P)
         )
 
+        eye_rows = held.tile([ROWS, ROWS], F32)
+        make_identity(nc, eye_rows[:])
         eye = held.tile([P, P], F32)
         make_identity(nc, eye[:])
         signs = held.tile([ROWS, WALKS, P], BF16)
         for c, (plus, minus) in enumerate(DIFFS):
             nc.vector.tensor_sub(
                 signs[:, c, :],
-                eye[0:ROWS, plus : plus + 1].to_broadcast([ROWS, P]),
-                eye[0:ROWS, minus : minus + 1].to_broadcast([ROWS, P]),
+                eye_rows[:, plus : plus + 1].to_broadcast([ROWS, P]),
+                eye_rows[:, minus : minus + 1].to_broadcast([ROWS, P]),
             )
         of_group = held.tile([P, P // LANES], F32)
         nc.vector.tensor_reduce(of_group[:], eye[:].rearrange("p (q s) -> p q s", s=LANES), axis=AX.X, op=ALU.add)

@@ -35,15 +35,16 @@ def tile_forestclf_kernel(tc, d, w_gate, b_gate, w_cls, b_cls, offs, out):
         tc.psum_pool(name="spread", bufs=WALKS * PIECES) as spread,
         tc.psum_pool(name="pack", bufs=1) as pack,
     ):
-        w_rows = held.tile([ROWS, N], BF16)
+        w_pair = [held.tile([2, N], BF16, name=f"w_pair_{c}") for c in range(WALKS)]
         d_bf = held.tile([P, S], BF16)
         offsets = held.tile([P, N // 16], U16, name="offsets")
         b_rows = held.tile([P, ROWS, T], F32)
-        nc.sync.dma_start(w_rows[0:2, :], w_gate)
-        nc.sync.dma_start(w_rows[2:5, :], w_cls)
+        nc.sync.dma_start(w_pair[0][:], w_cls[0:2, :])
         nc.scalar.dma_start(d_bf[:, HALF:S], d[:, HALF:S])
         nc.sync.dma_start(d_bf[:, 0:HALF], d[:, 0:HALF])
         nc.sync.dma_start(offsets[:], offs)
+        nc.sync.dma_start(w_pair[1][:], w_gate)
+        nc.sync.dma_start(w_pair[2][:], w_cls[0:3:2, :])
         nc.sync.dma_start(
             b_rows[:, 0:2, :].rearrange("p r t -> p (r t)"), b_gate.rearrange("r t -> (r t)").partition_broadcast(P)
         )
@@ -51,17 +52,11 @@ def tile_forestclf_kernel(tc, d, w_gate, b_gate, w_cls, b_cls, offs, out):
             b_rows[:, 2:5, :].rearrange("p r t -> p (r t)"), b_cls.rearrange("r t -> (r t)").partition_broadcast(P)
         )
 
-        eye_rows = held.tile([ROWS, ROWS], F32)
-        make_identity(nc, eye_rows[:])
+        signs = held.tile([2, P], BF16)
+        nc.vector.memset(signs[0:2, :], 1.0)
+        nc.vector.memset(signs[0:1, :], -1.0)
         eye = held.tile([P, P], F32)
         make_identity(nc, eye[:])
-        signs = held.tile([ROWS, WALKS, P], BF16)
-        for c, (plus, minus) in enumerate(DIFFS):
-            nc.vector.tensor_sub(
-                signs[:, c, :],
-                eye_rows[:, plus : plus + 1].to_broadcast([ROWS, P]),
-                eye_rows[:, minus : minus + 1].to_broadcast([ROWS, P]),
-            )
         of_group = held.tile([P, P // LANES], F32)
         nc.vector.tensor_reduce(of_group[:], eye[:].rearrange("p (q s) -> p q s", s=LANES), axis=AX.X, op=ALU.add)
         of_lane = held.tile([P, LANES], F32)
@@ -71,7 +66,7 @@ def tile_forestclf_kernel(tc, d, w_gate, b_gate, w_cls, b_cls, offs, out):
         for c in range(WALKS):
             for h in range(PIECES):
                 bank = spread.tile([P, PIECE], F32)
-                nc.tensor.matmul(bank[:], signs[:, c, :], w_rows[:, h * PIECE : (h + 1) * PIECE], start=True, stop=True)
+                nc.tensor.matmul(bank[:], signs[:], w_pair[c][:, h * PIECE : (h + 1) * PIECE], start=True, stop=True)
                 nc.scalar.copy(w_diff[c][h][:], bank[:])
 
         table = held.tile([P, S], F32)

@@ -43,14 +43,14 @@ def tile_forestclf_kernel(tc, d, w_gate, b_gate, w_cls, b_cls, offs, out):
         nc.scalar.dma_start(d_bf[:, HALF:S], d[:, HALF:S])
         nc.sync.dma_start(d_bf[:, 0:HALF], d[:, 0:HALF])
         nc.sync.dma_start(offsets[:], offs)
-        nc.sync.dma_start(w_pair[1][:], w_gate)
-        nc.sync.dma_start(w_pair[2][:], w_cls[0:3:2, :])
         nc.sync.dma_start(
             b_rows[:, 0:2, :].rearrange("p r t -> p (r t)"), b_gate.rearrange("r t -> (r t)").partition_broadcast(P)
         )
         nc.sync.dma_start(
             b_rows[:, 2:5, :].rearrange("p r t -> p (r t)"), b_cls.rearrange("r t -> (r t)").partition_broadcast(P)
         )
+        nc.sync.dma_start(w_pair[1][:], w_gate)
+        nc.sync.dma_start(w_pair[2][:], w_cls[0:3:2, :])
 
         signs = held.tile([2, P], BF16)
         nc.vector.memset(signs[0:2, :], 1.0)
@@ -75,9 +75,9 @@ def tile_forestclf_kernel(tc, d, w_gate, b_gate, w_cls, b_cls, offs, out):
 
         b_diff = held.tile([P, WALKS, T], F32)
         for c, (plus, minus) in enumerate(DIFFS):
-            nc.gpsimd.tensor_sub(b_diff[:, c, :], b_rows[:, plus, :], b_rows[:, minus, :])
+            nc.vector.tensor_sub(b_diff[:, c, :], b_rows[:, plus, :], b_rows[:, minus, :])
         b_part = held.tile([P, WALKS, T], F32)
-        nc.gpsimd.tensor_scalar_mul(b_part[:], b_diff[:], 1.0 / F)
+        nc.vector.tensor_scalar_mul(b_part[:], b_diff[:], 1.0 / F)
 
         score = held.tile([P, WALKS, T], F32)
 
@@ -112,11 +112,11 @@ def tile_forestclf_kernel(tc, d, w_gate, b_gate, w_cls, b_cls, offs, out):
         z1 = score[:, 0, :]
         cls_exp = exp_of_pair(z1, "cls")
         cls_sum = held.tile([P, T], F32)
-        nc.gpsimd.tensor_add(cls_sum[:], cls_exp[:, 0, :], cls_exp[:, 1, :])
+        nc.vector.tensor_add(cls_sum[:], cls_exp[:, 0, :], cls_exp[:, 1, :])
         top_part = held.tile([P, T], F32)
         nc.scalar.activation(top_part[:], z1, ACT.Relu, scale=1.0 / F)
         last_part = held.tile([P, T], F32)
-        nc.gpsimd.tensor_sub(last_part[:], b_part[:, 2, :], top_part[:])
+        nc.vector.tensor_sub(last_part[:], b_part[:, 2, :], top_part[:])
 
         walk_list(1, b_part[:, 1, :])
         gate_exp = exp_of_pair(score[:, 1, :], "gate")

@@ -17,7 +17,6 @@ F = N // T
 K = 3
 ROWS = 5
 WALKS = 3
-DIFFS = ((3, 2), (1, 0), (4, 2))
 PIECE = 512
 PIECES = N // PIECE
 TREES = PIECE // F
@@ -33,28 +32,32 @@ def tile_forestclf_kernel(tc, d, w_gate, b_gate, w_cls, b_cls, offs, out):
         tc.tile_pool(name="held", bufs=1) as held,
         tc.tile_pool(name="scrap", bufs=2) as scrap,
         tc.psum_pool(name="spread", bufs=WALKS * PIECES) as spread,
+        tc.psum_pool(name="spread_b", bufs=1) as spread_b,
         tc.psum_pool(name="pack", bufs=1) as pack,
     ):
         w_pair = [held.tile([2, N], BF16, name=f"w_pair_{c}") for c in range(WALKS)]
         d_bf = held.tile([P, S], BF16)
         offsets = held.tile([P, N // 16], U16, name="offsets")
-        b_rows = held.tile([P, ROWS, T], F32)
+        b_pair = held.tile([2, WALKS, T], F32)
         nc.sync.dma_start(w_pair[0][:], w_cls[0:2, :])
         nc.scalar.dma_start(d_bf[:, HALF:S], d[:, HALF:S])
         nc.sync.dma_start(d_bf[:, 0:HALF], d[:, 0:HALF])
         nc.sync.dma_start(offsets[:], offs)
-        nc.sync.dma_start(
-            b_rows[:, 0:2, :].rearrange("p r t -> p (r t)"), b_gate.rearrange("r t -> (r t)").partition_broadcast(P)
-        )
-        nc.sync.dma_start(
-            b_rows[:, 2:5, :].rearrange("p r t -> p (r t)"), b_cls.rearrange("r t -> (r t)").partition_broadcast(P)
-        )
         nc.sync.dma_start(w_pair[1][:], w_gate)
         nc.sync.dma_start(w_pair[2][:], w_cls[0:3:2, :])
+        nc.scalar.dma_start(b_pair[:, 0, :], b_cls[0:2, :])
+        nc.scalar.dma_start(b_pair[:, 1, :], b_gate)
+        nc.scalar.dma_start(b_pair[:, 2, :], b_cls[0:3:2, :])
 
         signs = held.tile([2, P], BF16)
         nc.vector.memset(signs[0:2, :], 1.0)
         nc.vector.memset(signs[0:1, :], -1.0)
+        signs_f32 = held.tile([2, P], F32)
+        nc.vector.memset(signs_f32[0:2, :], 1.0)
+        nc.vector.memset(signs_f32[0:1, :], -1.0)
+        flipped_f32 = held.tile([2, P], F32)
+        nc.vector.memset(flipped_f32[0:2, :], -1.0)
+        nc.vector.memset(flipped_f32[0:1, :], 1.0)
         eye = held.tile([P, P], F32)
         make_identity(nc, eye[:])
         of_group = held.tile([P, P // LANES], F32)
@@ -63,21 +66,30 @@ def tile_forestclf_kernel(tc, d, w_gate, b_gate, w_cls, b_cls, offs, out):
         nc.vector.tensor_reduce(of_lane[:], eye[:].rearrange("p (q s) -> p s q", s=LANES), axis=AX.X, op=ALU.add)
 
         w_diff = [[held.tile([P, PIECE], F32, name=f"w_diff_{c}_{h}") for h in range(PIECES)] for c in range(WALKS)]
-        for c in range(WALKS):
+
+        def spread_weights(c):
             for h in range(PIECES):
                 bank = spread.tile([P, PIECE], F32)
                 nc.tensor.matmul(bank[:], signs[:], w_pair[c][:, h * PIECE : (h + 1) * PIECE], start=True, stop=True)
                 nc.scalar.copy(w_diff[c][h][:], bank[:])
 
+        spread_weights(0)
+        spread_weights(1)
+
         table = held.tile([P, S], F32)
         nc.vector.tensor_copy(table[:, 0:HALF], d_bf[:, 0:HALF])
         nc.vector.tensor_copy(table[:, HALF:S], d_bf[:, HALF:S])
 
-        b_diff = held.tile([P, WALKS, T], F32)
-        for c, (plus, minus) in enumerate(DIFFS):
-            nc.vector.tensor_sub(b_diff[:, c, :], b_rows[:, plus, :], b_rows[:, minus, :])
-        b_part = held.tile([P, WALKS, T], F32)
-        nc.vector.tensor_scalar_mul(b_part[:], b_diff[:], 1.0 / F)
+        b_bank = spread_b.tile([P, WALKS, T], F32)
+        nc.tensor.matmul(
+            b_bank[:, 0:2, :].rearrange("p c t -> p (c t)"),
+            signs_f32[:],
+            b_pair[:, 0:2, :].rearrange("r c t -> r (c t)"),
+            start=True,
+            stop=True,
+        )
+        b_part = held.tile([P, 2, T], F32)
+        nc.scalar.activation(b_part[:], b_bank[:, 0:2, :], ACT.Copy, scale=1.0 / F)
 
         score = held.tile([P, WALKS, T], F32)
 
@@ -100,26 +112,29 @@ def tile_forestclf_kernel(tc, d, w_gate, b_gate, w_cls, b_cls, offs, out):
                         accum_out=score[:, c, t : t + 1],
                     )
 
-        def exp_of_pair(y, name):
-            arg = held.tile([P, 2, T], F32, name=f"{name}_arg")
-            nc.scalar.activation(arg[:, 0, :], y, ACT.Relu)
-            nc.scalar.activation(arg[:, 1, :], y, ACT.Relu, scale=-1.0)
+        def exp_of_pair(y, top, name):
+            nc.scalar.activation(top[:, 1, :], y, ACT.Relu, scale=-1.0)
             exps = held.tile([P, 2, T], F32, name=f"{name}_exp")
-            nc.scalar.activation(exps[:], arg[:], ACT.Exp, scale=-1.0)
+            nc.scalar.activation(exps[:], top[:], ACT.Exp, scale=-1.0)
             return exps
 
         walk_list(0, b_part[:, 0, :])
         z1 = score[:, 0, :]
-        cls_exp = exp_of_pair(z1, "cls")
+        cls_top = held.tile([P, 2, T], F32)
+        nc.scalar.activation(cls_top[:, 0, :], z1, ACT.Relu)
+        nc.tensor.matmul(b_bank[:, 2, :], flipped_f32[:], b_pair[:, 2, :], start=True, stop=False)
+        nc.tensor.matmul(b_bank[:, 2, :], eye[:], cls_top[:, 0, :], start=False, stop=True)
+        last_part = held.tile([P, T], F32)
+        nc.scalar.activation(last_part[:], b_bank[:, 2, :], ACT.Copy, scale=-1.0 / F)
+        spread_weights(2)
+        cls_exp = exp_of_pair(z1, cls_top, "cls")
         cls_sum = held.tile([P, T], F32)
         nc.vector.tensor_add(cls_sum[:], cls_exp[:, 0, :], cls_exp[:, 1, :])
-        top_part = held.tile([P, T], F32)
-        nc.scalar.activation(top_part[:], z1, ACT.Relu, scale=1.0 / F)
-        last_part = held.tile([P, T], F32)
-        nc.vector.tensor_sub(last_part[:], b_part[:, 2, :], top_part[:])
 
         walk_list(1, b_part[:, 1, :])
-        gate_exp = exp_of_pair(score[:, 1, :], "gate")
+        gate_top = held.tile([P, 2, T], F32)
+        nc.scalar.activation(gate_top[:, 0, :], score[:, 1, :], ACT.Relu)
+        gate_exp = exp_of_pair(score[:, 1, :], gate_top, "gate")
         gate_den = held.tile([P, T], F32)
         nc.vector.tensor_add(gate_den[:], gate_exp[:, 0, :], gate_exp[:, 1, :])
         gate_rec = held.tile([P, T], F32)

@@ -17,9 +17,10 @@ F = N // T
 K = 3
 ROWS = 5
 WALKS = 3
-PIECE = 512
-PIECES = N // PIECE
-TREES = PIECE // F
+BANK = 512
+BANKS = N // BANK
+EVEN_CUT = (BANK, BANK)
+LAST_CUT = (BANK, BANK // 2, F, F)
 LANES = 8
 CAP = 1.0e30
 
@@ -31,7 +32,7 @@ def tile_forestclf_kernel(tc, d, w_gate, b_gate, w_cls, b_cls, offs, out):
     with (
         tc.tile_pool(name="held", bufs=1) as held,
         tc.tile_pool(name="scrap", bufs=2) as scrap,
-        tc.psum_pool(name="spread", bufs=WALKS * PIECES) as spread,
+        tc.psum_pool(name="spread", bufs=WALKS * BANKS) as spread,
         tc.psum_pool(name="spread_b", bufs=1) as spread_b,
         tc.psum_pool(name="pack", bufs=1) as pack,
     ):
@@ -64,17 +65,23 @@ def tile_forestclf_kernel(tc, d, w_gate, b_gate, w_cls, b_cls, offs, out):
         nc.vector.tensor_reduce(of_group[:], eye[:].rearrange("p (q s) -> p q s", s=LANES), axis=AX.X, op=ALU.add)
         of_lane = held.tile([P, LANES], F32)
         nc.vector.tensor_reduce(of_lane[:], eye[:].rearrange("p (q s) -> p s q", s=LANES), axis=AX.X, op=ALU.add)
+        third_one = held.tile([P // LANES, LANES, K], F32)
+        nc.vector.memset(third_one[:], 0.0)
+        nc.vector.memset(third_one[:, :, K - 1], 1.0)
 
-        w_diff = [[held.tile([P, PIECE], F32, name=f"w_diff_{c}_{h}") for h in range(PIECES)] for c in range(WALKS)]
+        w_diff = [[held.tile([P, BANK], F32, name=f"w_diff_{c}_{h}") for h in range(BANKS)] for c in range(WALKS)]
 
-        def spread_weights(c):
-            for h in range(PIECES):
-                bank = spread.tile([P, PIECE], F32)
-                nc.tensor.matmul(bank[:], signs[:], w_pair[c][:, h * PIECE : (h + 1) * PIECE], start=True, stop=True)
-                nc.scalar.copy(w_diff[c][h][:], bank[:])
+        def spread_weights(c, cut):
+            first = 0
+            for size in cut:
+                h, at = divmod(first, BANK)
+                bank = spread.tile([P, size], F32, tag="bank")
+                nc.tensor.matmul(bank[:], signs[:], w_pair[c][:, first : first + size], start=True, stop=True)
+                nc.scalar.copy(w_diff[c][h][:, at : at + size], bank[:])
+                first += size
 
-        spread_weights(0)
-        spread_weights(1)
+        spread_weights(0, (BANK // 2, BANK // 2, BANK))
+        spread_weights(1, EVEN_CUT)
 
         table = held.tile([P, S], F32)
         nc.vector.tensor_copy(table[:, 0:HALF], d_bf[:, 0:HALF])
@@ -93,32 +100,33 @@ def tile_forestclf_kernel(tc, d, w_gate, b_gate, w_cls, b_cls, offs, out):
 
         score = held.tile([P, WALKS, T], F32)
 
-        def walk_list(c, part):
-            for h in range(PIECES):
-                prod = held.tile([P, PIECE], F32, name=f"prod_{c}_{h}")
+        def walk_list(c, part, cut):
+            first = 0
+            for size in cut:
+                h, at = divmod(first, BANK)
+                prod = held.tile([P, size], F32, name=f"prod_{c}_{first}")
                 nc.vector.tensor_tensor(
                     prod[:],
-                    table[:].indirect(offsets[:, h * (PIECE // 16) : (h + 1) * (PIECE // 16)]),
-                    w_diff[c][h][:],
+                    table[:].indirect(offsets[:, first // 16 : (first + size) // 16]),
+                    w_diff[c][h][:, at : at + size],
                     ALU.mult,
                 )
-                for t in range(h * TREES, (h + 1) * TREES):
+                for t in range(first // F, (first + size) // F):
                     unused = scrap.tile([P, F], F32)
                     nc.scalar.activation(
                         unused[:],
-                        prod[:, (t - h * TREES) * F : (t - h * TREES + 1) * F],
+                        prod[:, t * F - first : (t + 1) * F - first],
                         ACT.Identity,
                         bias=part[:, t : t + 1],
                         accum_out=score[:, c, t : t + 1],
                     )
+                first += size
 
-        def exp_of_pair(y, top, name):
+        def exp_of_pair(exps, y, top):
             nc.scalar.activation(top[:, 1, :], y, ACT.Relu, scale=-1.0)
-            exps = held.tile([P, 2, T], F32, name=f"{name}_exp")
-            nc.scalar.activation(exps[:], top[:], ACT.Exp, scale=-1.0)
-            return exps
+            nc.scalar.activation(exps, top[:], ACT.Exp, scale=-1.0)
 
-        walk_list(0, b_part[:, 0, :])
+        walk_list(0, b_part[:, 0, :], EVEN_CUT)
         z1 = score[:, 0, :]
         cls_top = held.tile([P, 2, T], F32)
         nc.scalar.activation(cls_top[:, 0, :], z1, ACT.Relu)
@@ -126,36 +134,32 @@ def tile_forestclf_kernel(tc, d, w_gate, b_gate, w_cls, b_cls, offs, out):
         nc.tensor.matmul(b_bank[:, 2, :], eye[:], cls_top[:, 0, :], start=False, stop=True)
         last_part = held.tile([P, T], F32)
         nc.scalar.activation(last_part[:], b_bank[:, 2, :], ACT.Copy, scale=-1.0 / F)
-        spread_weights(2)
-        cls_exp = exp_of_pair(z1, cls_top, "cls")
-        cls_sum = held.tile([P, T], F32)
-        nc.vector.tensor_add(cls_sum[:], cls_exp[:, 0, :], cls_exp[:, 1, :])
+        spread_weights(2, EVEN_CUT)
+        cls_exp = held.tile([P, K, T], F32)
+        exp_of_pair(cls_exp[:, 0:2, :], z1, cls_top)
+        nc.vector.scalar_tensor_tensor(cls_exp[:, 2, :], cls_exp[:, 0, :], -1.0, cls_exp[:, 1, :], ALU.mult, ALU.subtract)
 
-        walk_list(1, b_part[:, 1, :])
-        gate_top = held.tile([P, 2, T], F32)
-        nc.scalar.activation(gate_top[:, 0, :], score[:, 1, :], ACT.Relu)
-        gate_exp = exp_of_pair(score[:, 1, :], gate_top, "gate")
+        walk_list(1, b_part[:, 1, :], EVEN_CUT)
+        gate_exp = held.tile([P, T], F32)
+        nc.scalar.activation(gate_exp[:], score[:, 1, :], ACT.Exp, scale=-1.0)
         gate_den = held.tile([P, T], F32)
-        nc.vector.tensor_add(gate_den[:], gate_exp[:, 0, :], gate_exp[:, 1, :])
-        gate_rec = held.tile([P, T], F32)
-        nc.vector.reciprocal(gate_rec[:], gate_den[:])
+        nc.vector.tensor_scalar(gate_den[:], gate_exp[:], CAP, 1.0, ALU.min, ALU.add)
         gate = held.tile([P, T], F32)
-        nc.vector.tensor_mul(gate[:], gate_exp[:, 1, :], gate_rec[:])
-        gated = held.tile([P, K, T], F32)
-        nc.vector.tensor_mul(gated[:, 0:2, :], cls_exp[:], gate[:].unsqueeze(1).to_broadcast([P, 2, T]))
+        nc.vector.reciprocal(gate[:], gate_den[:])
         gate_sum = held.tile([P, 1], F32)
         nc.vector.tensor_reduce(gate_sum[:], gate[:], axis=AX.X, op=ALU.add)
         gate_sum_rec = held.tile([P, 1], F32)
         nc.vector.reciprocal(gate_sum_rec[:], gate_sum[:])
-        lane_share = held.tile([P, LANES], F32)
-        nc.vector.tensor_scalar_mul(lane_share[:], of_lane[:], gate_sum_rec[:])
+        gated = held.tile([P, K, T], F32)
+        nc.vector.scalar_tensor_tensor(
+            gated[:], cls_exp[:], gate_sum_rec[:], gate[:].unsqueeze(1).to_broadcast([P, K, T]), ALU.mult, ALU.mult
+        )
 
-        walk_list(2, last_part[:])
+        walk_list(2, last_part[:], LAST_CUT)
         last_exp = held.tile([P, T], F32)
         nc.scalar.activation(last_exp[:], score[:, 2, :], ACT.Exp)
         cls_den = held.tile([P, T], F32)
-        nc.vector.scalar_tensor_tensor(cls_den[:], last_exp[:], CAP, cls_sum[:], ALU.min, ALU.add)
-        nc.vector.scalar_tensor_tensor(gated[:, 2, :], last_exp[:], CAP, gate[:], ALU.min, ALU.mult)
+        nc.vector.scalar_tensor_tensor(cls_den[:], last_exp[:], CAP, cls_exp[:, 2, :], ALU.min, ALU.subtract)
         cls_rec = held.tile([P, T], F32)
         nc.vector.reciprocal(cls_rec[:], cls_den[:])
         weighted = held.tile([P, K, T], F32)
@@ -166,11 +170,11 @@ def tile_forestclf_kernel(tc, d, w_gate, b_gate, w_cls, b_cls, offs, out):
         blocks = held.tile([P, LANES, K], F32)
         nc.vector.tensor_mul(
             blocks[:],
-            lane_share[:].unsqueeze(2).to_broadcast([P, LANES, K]),
+            of_lane[:].unsqueeze(2).to_broadcast([P, LANES, K]),
             total[:].unsqueeze(1).to_broadcast([P, LANES, K]),
         )
         packed_ps = pack.tile([P // LANES, LANES * K], F32)
         nc.tensor.matmul(packed_ps[:], of_group[:], blocks[:].rearrange("p s k -> p (s k)"), start=True, stop=True)
         packed = held.tile([P // LANES, LANES * K], F32)
-        nc.vector.tensor_copy(packed[:], packed_ps[:])
+        nc.vector.tensor_add(packed[:], packed_ps[:], third_one[:].rearrange("q s k -> q (s k)"))
         nc.sync.dma_start(out.rearrange("(q s) k -> q (s k)", s=LANES), packed[:])

@@ -135,25 +135,25 @@ def tile_forestclf_kernel(tc, d, w_gate, b_gate, w_cls, b_cls, offs, out):
         last_part = held.tile([P, T], F32)
         nc.scalar.activation(last_part[:], b_bank[:, 2, :], ACT.Copy, scale=-1.0 / F)
         spread_weights(2, EVEN_CUT)
-        cls_exp = held.tile([P, K, T], F32)
-        exp_of_pair(cls_exp[:, 0:2, :], z1, cls_top)
-        nc.vector.scalar_tensor_tensor(cls_exp[:, 2, :], cls_exp[:, 0, :], -1.0, cls_exp[:, 1, :], ALU.mult, ALU.subtract)
 
         walk_list(1, b_part[:, 1, :], EVEN_CUT)
         gate_exp = held.tile([P, T], F32)
         nc.scalar.activation(gate_exp[:], score[:, 1, :], ACT.Exp, scale=-1.0)
+        cls_exp = held.tile([P, K, T], F32)
+        exp_of_pair(cls_exp[:, 0:2, :], z1, cls_top)
         gate_den = held.tile([P, T], F32)
         nc.vector.tensor_scalar(gate_den[:], gate_exp[:], CAP, 1.0, ALU.min, ALU.add)
         gate = held.tile([P, T], F32)
         nc.vector.reciprocal(gate[:], gate_den[:])
+        nc.vector.scalar_tensor_tensor(cls_exp[:, 2, :], cls_exp[:, 0, :], -1.0, cls_exp[:, 1, :], ALU.mult, ALU.subtract)
+        gated = held.tile([P, K, T], F32)
+        nc.vector.tensor_mul(gated[:], cls_exp[:], gate[:].unsqueeze(1).to_broadcast([P, K, T]))
         gate_sum = held.tile([P, 1], F32)
         nc.vector.tensor_reduce(gate_sum[:], gate[:], axis=AX.X, op=ALU.add)
         gate_sum_rec = held.tile([P, 1], F32)
         nc.vector.reciprocal(gate_sum_rec[:], gate_sum[:])
-        gated = held.tile([P, K, T], F32)
-        nc.vector.scalar_tensor_tensor(
-            gated[:], cls_exp[:], gate_sum_rec[:], gate[:].unsqueeze(1).to_broadcast([P, K, T]), ALU.mult, ALU.mult
-        )
+        lane_share = held.tile([P, LANES], F32)
+        nc.vector.tensor_scalar_mul(lane_share[:], of_lane[:], gate_sum_rec[:])
 
         walk_list(2, last_part[:], LAST_CUT)
         last_exp = held.tile([P, T], F32)
@@ -170,7 +170,7 @@ def tile_forestclf_kernel(tc, d, w_gate, b_gate, w_cls, b_cls, offs, out):
         blocks = held.tile([P, LANES, K], F32)
         nc.vector.tensor_mul(
             blocks[:],
-            of_lane[:].unsqueeze(2).to_broadcast([P, LANES, K]),
+            lane_share[:].unsqueeze(2).to_broadcast([P, LANES, K]),
             total[:].unsqueeze(1).to_broadcast([P, LANES, K]),
         )
         packed_ps = pack.tile([P // LANES, LANES * K], F32)

@@ -45,10 +45,10 @@ def tile_forestclf_kernel(tc, d, w_gate, b_gate, w_cls, b_cls, offs, out):
         nc.sync.dma_start(d_bf[:, 0:HALF], d[:, 0:HALF])
         nc.sync.dma_start(offsets[:], offs)
         nc.sync.dma_start(w_pair[1][:], w_gate)
+        nc.sync.dma_start(b_pair[:, 2, :], b_cls[0:3:2, :])
         nc.sync.dma_start(w_pair[2][:], w_cls[0:3:2, :])
         nc.scalar.dma_start(b_pair[:, 0, :], b_cls[0:2, :])
         nc.scalar.dma_start(b_pair[:, 1, :], b_gate)
-        nc.scalar.dma_start(b_pair[:, 2, :], b_cls[0:3:2, :])
 
         signs = held.tile([2, P], BF16)
         nc.vector.memset(signs[0:2, :], 1.0)

@@ -44,11 +44,11 @@ def tile_forestclf_kernel(tc, d, w_gate, b_gate, w_cls, b_cls, offs, out):
         nc.scalar.dma_start(d_bf[:, HALF:S], d[:, HALF:S])
         nc.sync.dma_start(d_bf[:, 0:HALF], d[:, 0:HALF])
         nc.sync.dma_start(offsets[:], offs)
-        nc.sync.dma_start(w_pair[1][:], w_gate)
+        nc.scalar.dma_start(w_pair[1][:], w_gate)
+        nc.sync.dma_start(b_pair[:, 0, :], b_cls[0:2, :])
+        nc.sync.dma_start(b_pair[:, 1, :], b_gate)
         nc.sync.dma_start(b_pair[:, 2, :], b_cls[0:3:2, :])
         nc.sync.dma_start(w_pair[2][:], w_cls[0:3:2, :])
-        nc.scalar.dma_start(b_pair[:, 0, :], b_cls[0:2, :])
-        nc.scalar.dma_start(b_pair[:, 1, :], b_gate)
 
         signs = held.tile([2, P], BF16)
         nc.vector.memset(signs[0:2, :], 1.0)

@@ -31,7 +31,6 @@ def tile_forestclf_kernel(tc, d, w_gate, b_gate, w_cls, b_cls, offs, out):
     nc = tc.nc
     with (
         tc.tile_pool(name="held", bufs=1) as held,
-        tc.tile_pool(name="scrap", bufs=2) as scrap,
         tc.psum_pool(name="spread", bufs=WALKS * BANKS) as spread,
         tc.psum_pool(name="spread_b", bufs=1) as spread_b,
         tc.psum_pool(name="pack", bufs=1) as pack,
@@ -112,9 +111,8 @@ def tile_forestclf_kernel(tc, d, w_gate, b_gate, w_cls, b_cls, offs, out):
                     ALU.mult,
                 )
                 for t in range(first // F, (first + size) // F):
-                    unused = scrap.tile([P, F], F32)
                     nc.scalar.activation(
-                        unused[:],
+                        prod[:, t * F - first : (t + 1) * F - first],
                         prod[:, t * F - first : (t + 1) * F - first],
                         ACT.Identity,
                         bias=part[:, t : t + 1],
@@ -132,17 +130,17 @@ def tile_forestclf_kernel(tc, d, w_gate, b_gate, w_cls, b_cls, offs, out):
         nc.scalar.activation(cls_top[:, 0, :], z1, ACT.Relu)
         nc.tensor.matmul(b_bank[:, 2, :], flipped_f32[:], b_pair[:, 2, :], start=True, stop=False)
         nc.tensor.matmul(b_bank[:, 2, :], eye[:], cls_top[:, 0, :], start=False, stop=True)
-        last_part = held.tile([P, T], F32)
-        nc.scalar.activation(last_part[:], b_bank[:, 2, :], ACT.Copy, scale=-1.0 / F)
         spread_weights(2, EVEN_CUT)
 
         walk_list(1, b_part[:, 1, :], EVEN_CUT)
+        last_part = held.tile([P, T], F32)
+        nc.scalar.activation(last_part[:], b_bank[:, 2, :], ACT.Copy, scale=-1.0 / F)
         gate_exp = held.tile([P, T], F32)
         nc.scalar.activation(gate_exp[:], score[:, 1, :], ACT.Exp, scale=-1.0)
+        gate_den = held.tile([P, T], F32)
+        nc.scalar.activation(gate_den[:], gate_exp[:], ACT.Copy, bias=1.0)
         cls_exp = held.tile([P, K, T], F32)
         exp_of_pair(cls_exp[:, 0:2, :], z1, cls_top)
-        gate_den = held.tile([P, T], F32)
-        nc.vector.tensor_scalar(gate_den[:], gate_exp[:], CAP, 1.0, ALU.min, ALU.add)
         gate = held.tile([P, T], F32)
         nc.vector.reciprocal(gate[:], gate_den[:])
         nc.vector.scalar_tensor_tensor(cls_exp[:, 2, :], cls_exp[:, 0, :], -1.0, cls_exp[:, 1, :], ALU.mult, ALU.subtract)
@@ -152,8 +150,6 @@ def tile_forestclf_kernel(tc, d, w_gate, b_gate, w_cls, b_cls, offs, out):
         nc.vector.tensor_reduce(gate_sum[:], gate[:], axis=AX.X, op=ALU.add)
         gate_sum_rec = held.tile([P, 1], F32)
         nc.vector.reciprocal(gate_sum_rec[:], gate_sum[:])
-        lane_share = held.tile([P, LANES], F32)
-        nc.vector.tensor_scalar_mul(lane_share[:], of_lane[:], gate_sum_rec[:])
 
         walk_list(2, last_part[:], LAST_CUT)
         last_exp = held.tile([P, T], F32)
@@ -168,10 +164,13 @@ def tile_forestclf_kernel(tc, d, w_gate, b_gate, w_cls, b_cls, offs, out):
         nc.vector.tensor_reduce(total[:], weighted[:], axis=AX.X, op=ALU.add)
 
         blocks = held.tile([P, LANES, K], F32)
-        nc.vector.tensor_mul(
+        nc.vector.scalar_tensor_tensor(
             blocks[:],
-            lane_share[:].unsqueeze(2).to_broadcast([P, LANES, K]),
+            of_lane[:].unsqueeze(2).to_broadcast([P, LANES, K]),
+            gate_sum_rec[:],
             total[:].unsqueeze(1).to_broadcast([P, LANES, K]),
+            ALU.mult,
+            ALU.mult,
         )
         packed_ps = pack.tile([P // LANES, LANES * K], F32)
         nc.tensor.matmul(packed_ps[:], of_group[:], blocks[:].rearrange("p s k -> p (s k)"), start=True, stop=True)

@@ -43,7 +43,7 @@ def tile_forestclf_kernel(tc, d, w_gate, b_gate, w_cls, b_cls, offs, out):
         nc.scalar.dma_start(d_bf[:, HALF:S], d[:, HALF:S])
         nc.sync.dma_start(d_bf[:, 0:HALF], d[:, 0:HALF])
         nc.sync.dma_start(offsets[:], offs)
-        nc.scalar.dma_start(w_pair[1][:], w_gate)
+        nc.gpsimd.dma_start(w_pair[1][:], w_gate)
         nc.sync.dma_start(b_pair[:, 0, :], b_cls[0:2, :])
         nc.sync.dma_start(b_pair[:, 1, :], b_gate)
         nc.sync.dma_start(b_pair[:, 2, :], b_cls[0:3:2, :])

@@ -20,7 +20,6 @@ WALKS = 3
 BANK = 512
 BANKS = N // BANK
 EVEN_CUT = (BANK, BANK)
-LAST_CUT = (BANK, BANK // 2, F, F)
 LANES = 8
 CAP = 1.0e30
 
@@ -97,9 +96,7 @@ def tile_forestclf_kernel(tc, d, w_gate, b_gate, w_cls, b_cls, offs, out):
         b_part = held.tile([P, 2, T], F32)
         nc.scalar.activation(b_part[:], b_bank[:, 0:2, :], ACT.Copy, scale=1.0 / F)
 
-        score = held.tile([P, WALKS, T], F32)
-
-        def walk_list(c, part, cut):
+        def walk_list(c, part, cut, score):
             first = 0
             for size in cut:
                 h, at = divmod(first, BANK)
@@ -116,44 +113,44 @@ def tile_forestclf_kernel(tc, d, w_gate, b_gate, w_cls, b_cls, offs, out):
                         prod[:, t * F - first : (t + 1) * F - first],
                         ACT.Identity,
                         bias=part[:, t : t + 1],
-                        accum_out=score[:, c, t : t + 1],
+                        accum_out=score[:, t : t + 1],
                     )
                 first += size
 
-        def exp_of_pair(exps, y, top):
-            nc.scalar.activation(top[:, 1, :], y, ACT.Relu, scale=-1.0)
-            nc.scalar.activation(exps, top[:], ACT.Exp, scale=-1.0)
+        early_arg = held.tile([P, 1 + 2, T], F32)
+        x = early_arg[:, 0, :]
+        cls_top = early_arg[:, 1, :]
 
-        walk_list(0, b_part[:, 0, :], EVEN_CUT)
-        z1 = score[:, 0, :]
-        cls_top = held.tile([P, 2, T], F32)
-        nc.scalar.activation(cls_top[:, 0, :], z1, ACT.Relu)
+        z1 = held.tile([P, T], F32)
+        walk_list(0, b_part[:, 0, :], EVEN_CUT, z1)
+        nc.scalar.activation(cls_top, z1[:], ACT.Relu)
         nc.tensor.matmul(b_bank[:, 2, :], flipped_f32[:], b_pair[:, 2, :], start=True, stop=False)
-        nc.tensor.matmul(b_bank[:, 2, :], eye[:], cls_top[:, 0, :], start=False, stop=True)
+        nc.tensor.matmul(b_bank[:, 2, :], eye[:], cls_top, start=False, stop=True)
+        nc.scalar.activation(early_arg[:, 2, :], z1[:], ACT.Relu, scale=-1.0)
         spread_weights(2, EVEN_CUT)
 
-        walk_list(1, b_part[:, 1, :], EVEN_CUT)
+        walk_list(1, b_part[:, 1, :], EVEN_CUT, x)
         last_part = held.tile([P, T], F32)
         nc.scalar.activation(last_part[:], b_bank[:, 2, :], ACT.Copy, scale=-1.0 / F)
-        gate_exp = held.tile([P, T], F32)
-        nc.scalar.activation(gate_exp[:], score[:, 1, :], ACT.Exp, scale=-1.0)
+        early_exp = held.tile([P, 1 + K, T], F32)
+        nc.scalar.activation(early_exp[:, 0 : 1 + 2, :], early_arg[:], ACT.Exp, scale=-1.0)
+        cls_exp = early_exp[:, 1 : 1 + K, :]
         gate_den = held.tile([P, T], F32)
-        nc.scalar.activation(gate_den[:], gate_exp[:], ACT.Copy, bias=1.0)
-        cls_exp = held.tile([P, K, T], F32)
-        exp_of_pair(cls_exp[:, 0:2, :], z1, cls_top)
+        nc.scalar.activation(gate_den[:], early_exp[:, 0, :], ACT.Copy, bias=1.0)
         gate = held.tile([P, T], F32)
         nc.vector.reciprocal(gate[:], gate_den[:])
         nc.vector.scalar_tensor_tensor(cls_exp[:, 2, :], cls_exp[:, 0, :], -1.0, cls_exp[:, 1, :], ALU.mult, ALU.subtract)
         gated = held.tile([P, K, T], F32)
-        nc.vector.tensor_mul(gated[:], cls_exp[:], gate[:].unsqueeze(1).to_broadcast([P, K, T]))
+        nc.vector.tensor_mul(gated[:], cls_exp, gate[:].unsqueeze(1).to_broadcast([P, K, T]))
         gate_sum = held.tile([P, 1], F32)
         nc.vector.tensor_reduce(gate_sum[:], gate[:], axis=AX.X, op=ALU.add)
         gate_sum_rec = held.tile([P, 1], F32)
         nc.vector.reciprocal(gate_sum_rec[:], gate_sum[:])
 
-        walk_list(2, last_part[:], LAST_CUT)
+        last_arg = held.tile([P, T], F32)
+        walk_list(2, last_part[:], EVEN_CUT, last_arg)
         last_exp = held.tile([P, T], F32)
-        nc.scalar.activation(last_exp[:], score[:, 2, :], ACT.Exp)
+        nc.scalar.activation(last_exp[:], last_arg[:], ACT.Exp)
         cls_den = held.tile([P, T], F32)
         nc.vector.scalar_tensor_tensor(cls_den[:], last_exp[:], CAP, cls_exp[:, 2, :], ALU.min, ALU.subtract)
         cls_rec = held.tile([P, T], F32)

@@ -108,13 +108,15 @@ def tile_forestclf_kernel(tc, d, w_gate, b_gate, w_cls, b_cls, offs, out):
                     ALU.mult,
                 )
                 for t in range(first // F, (first + size) // F):
-                    nc.scalar.activation(
-                        prod[:, t * F - first : (t + 1) * F - first],
-                        prod[:, t * F - first : (t + 1) * F - first],
-                        ACT.Identity,
-                        bias=part[:, t : t + 1],
-                        accum_out=score[:, t : t + 1],
-                    )
+                    of_tree = prod[:, t * F - first : (t + 1) * F - first]
+                    if (c, t) == (WALKS - 1, T - 1):
+                        nc.vector.tensor_scalar(
+                            of_tree, of_tree, part[:, t : t + 1], None, ALU.add, ALU.add, accum_out=score[:, t : t + 1]
+                        )
+                    else:
+                        nc.scalar.activation(
+                            of_tree, of_tree, ACT.Identity, bias=part[:, t : t + 1], accum_out=score[:, t : t + 1]
+                        )
                 first += size
 
         early_arg = held.tile([P, 1 + 2, T], F32)

import concourse.mybir as mybir
from concourse.masks import make_identity

F32 = mybir.dt.float32
BF16 = mybir.dt.bfloat16
U16 = mybir.dt.uint16
ALU = mybir.AluOpType
ACT = mybir.ActivationFunctionType
AX = mybir.AxisListType

P = 128
S = 1024
HALF = S // 2
N = 1024
T = 8
F = N // T
K = 3
ROWS = 5
WALKS = 3
BANK = 512
BANKS = N // BANK
EVEN_CUT = (BANK, BANK)
LANES = 8
CAP = 1.0e30

FLOPS = 2 * P * N * ROWS


def tile_forestclf_kernel(tc, d, w_gate, b_gate, w_cls, b_cls, offs, out):
    nc = tc.nc
    with (
        tc.tile_pool(name="held", bufs=1) as held,
        tc.psum_pool(name="spread", bufs=WALKS * BANKS) as spread,
        tc.psum_pool(name="spread_b", bufs=1) as spread_b,
        tc.psum_pool(name="pack", bufs=1) as pack,
    ):
        w_pair = [held.tile([2, N], BF16, name=f"w_pair_{c}") for c in range(WALKS)]
        d_bf = held.tile([P, S], BF16)
        offsets = held.tile([P, N // 16], U16, name="offsets")
        b_pair = held.tile([2, WALKS, T], F32)
        nc.sync.dma_start(w_pair[0][:], w_cls[0:2, :])
        nc.scalar.dma_start(d_bf[:, HALF:S], d[:, HALF:S])
        nc.sync.dma_start(d_bf[:, 0:HALF], d[:, 0:HALF])
        nc.sync.dma_start(offsets[:], offs)
        nc.gpsimd.dma_start(w_pair[1][:], w_gate)
        nc.sync.dma_start(b_pair[:, 0, :], b_cls[0:2, :])
        nc.sync.dma_start(b_pair[:, 1, :], b_gate)
        nc.sync.dma_start(b_pair[:, 2, :], b_cls[0:3:2, :])
        nc.sync.dma_start(w_pair[2][:], w_cls[0:3:2, :])

        signs = held.tile([2, P], BF16)
        nc.vector.memset(signs[0:2, :], 1.0)
        nc.vector.memset(signs[0:1, :], -1.0)
        signs_f32 = held.tile([2, P], F32)
        nc.vector.memset(signs_f32[0:2, :], 1.0)
        nc.vector.memset(signs_f32[0:1, :], -1.0)
        flipped_f32 = held.tile([2, P], F32)
        nc.vector.memset(flipped_f32[0:2, :], -1.0)
        nc.vector.memset(flipped_f32[0:1, :], 1.0)
        eye = held.tile([P, P], F32)
        make_identity(nc, eye[:])
        of_group = held.tile([P, P // LANES], F32)
        nc.vector.tensor_reduce(of_group[:], eye[:].rearrange("p (q s) -> p q s", s=LANES), axis=AX.X, op=ALU.add)
        of_lane = held.tile([P, LANES], F32)
        nc.vector.tensor_reduce(of_lane[:], eye[:].rearrange("p (q s) -> p s q", s=LANES), axis=AX.X, op=ALU.add)
        third_one = held.tile([P // LANES, LANES, K], F32)
        nc.vector.memset(third_one[:], 0.0)
        nc.vector.memset(third_one[:, :, K - 1], 1.0)

        w_diff = [[held.tile([P, BANK], F32, name=f"w_diff_{c}_{h}") for h in range(BANKS)] for c in range(WALKS)]

        def spread_weights(c, cut):
            first = 0
            for size in cut:
                h, at = divmod(first, BANK)
                bank = spread.tile([P, size], F32, tag="bank")
                nc.tensor.matmul(bank[:], signs[:], w_pair[c][:, first : first + size], start=True, stop=True)
                nc.scalar.copy(w_diff[c][h][:, at : at + size], bank[:])
                first += size

        spread_weights(0, (BANK // 2, BANK // 2, BANK))
        spread_weights(1, EVEN_CUT)

        table = held.tile([P, S], F32)
        nc.vector.tensor_copy(table[:, 0:HALF], d_bf[:, 0:HALF])
        nc.vector.tensor_copy(table[:, HALF:S], d_bf[:, HALF:S])

        b_bank = spread_b.tile([P, WALKS, T], F32)
        nc.tensor.matmul(
            b_bank[:, 0:2, :].rearrange("p c t -> p (c t)"),
            signs_f32[:],
            b_pair[:, 0:2, :].rearrange("r c t -> r (c t)"),
            start=True,
            stop=True,
        )
        b_part = held.tile([P, 2, T], F32)
        nc.scalar.activation(b_part[:], b_bank[:, 0:2, :], ACT.Copy, scale=1.0 / F)

        def walk_list(c, part, cut, score):
            first = 0
            for size in cut:
                h, at = divmod(first, BANK)
                prod = held.tile([P, size], F32, name=f"prod_{c}_{first}")
                nc.vector.tensor_tensor(
                    prod[:],
                    table[:].indirect(offsets[:, first // 16 : (first + size) // 16]),
                    w_diff[c][h][:, at : at + size],
                    ALU.mult,
                )
                for t in range(first // F, (first + size) // F):
                    of_tree = prod[:, t * F - first : (t + 1) * F - first]
                    if (c, t) == (WALKS - 1, T - 1):
                        nc.vector.tensor_scalar(
                            of_tree, of_tree, part[:, t : t + 1], None, ALU.add, ALU.add, accum_out=score[:, t : t + 1]
                        )
                    else:
                        nc.scalar.activation(
                            of_tree, of_tree, ACT.Identity, bias=part[:, t : t + 1], accum_out=score[:, t : t + 1]
                        )
                first += size

        early_arg = held.tile([P, 1 + 2, T], F32)
        x = early_arg[:, 0, :]
        cls_top = early_arg[:, 1, :]

        z1 = held.tile([P, T], F32)
        walk_list(0, b_part[:, 0, :], EVEN_CUT, z1)
        nc.scalar.activation(cls_top, z1[:], ACT.Relu)
        nc.tensor.matmul(b_bank[:, 2, :], flipped_f32[:], b_pair[:, 2, :], start=True, stop=False)
        nc.tensor.matmul(b_bank[:, 2, :], eye[:], cls_top, start=False, stop=True)
        nc.scalar.activation(early_arg[:, 2, :], z1[:], ACT.Relu, scale=-1.0)
        spread_weights(2, EVEN_CUT)

        walk_list(1, b_part[:, 1, :], EVEN_CUT, x)
        last_part = held.tile([P, T], F32)
        nc.scalar.activation(last_part[:], b_bank[:, 2, :], ACT.Copy, scale=-1.0 / F)
        early_exp = held.tile([P, 1 + K, T], F32)
        nc.scalar.activation(early_exp[:, 0 : 1 + 2, :], early_arg[:], ACT.Exp, scale=-1.0)
        cls_exp = early_exp[:, 1 : 1 + K, :]
        gate_den = held.tile([P, T], F32)
        nc.scalar.activation(gate_den[:], early_exp[:, 0, :], ACT.Copy, bias=1.0)
        gate = held.tile([P, T], F32)
        nc.vector.reciprocal(gate[:], gate_den[:])
        nc.vector.scalar_tensor_tensor(cls_exp[:, 2, :], cls_exp[:, 0, :], -1.0, cls_exp[:, 1, :], ALU.mult, ALU.subtract)
        gated = held.tile([P, K, T], F32)
        nc.vector.tensor_mul(gated[:], cls_exp, gate[:].unsqueeze(1).to_broadcast([P, K, T]))
        gate_sum = held.tile([P, 1], F32)
        nc.vector.tensor_reduce(gate_sum[:], gate[:], axis=AX.X, op=ALU.add)
        gate_sum_rec = held.tile([P, 1], F32)
        nc.vector.reciprocal(gate_sum_rec[:], gate_sum[:])

        last_arg = held.tile([P, T], F32)
        walk_list(2, last_part[:], EVEN_CUT, last_arg)
        last_exp = held.tile([P, T], F32)
        nc.scalar.activation(last_exp[:], last_arg[:], ACT.Exp)
        cls_den = held.tile([P, T], F32)
        nc.vector.scalar_tensor_tensor(cls_den[:], last_exp[:], CAP, cls_exp[:, 2, :], ALU.min, ALU.subtract)
        cls_rec = held.tile([P, T], F32)
        nc.vector.reciprocal(cls_rec[:], cls_den[:])
        weighted = held.tile([P, K, T], F32)
        nc.vector.tensor_mul(weighted[:], gated[:], cls_rec[:].unsqueeze(1).to_broadcast([P, K, T]))
        total = held.tile([P, K], F32)
        nc.vector.tensor_reduce(total[:], weighted[:], axis=AX.X, op=ALU.add)

        blocks = held.tile([P, LANES, K], F32)
        nc.vector.scalar_tensor_tensor(
            blocks[:],
            of_lane[:].unsqueeze(2).to_broadcast([P, LANES, K]),
            gate_sum_rec[:],
            total[:].unsqueeze(1).to_broadcast([P, LANES, K]),
            ALU.mult,
            ALU.mult,
        )
        packed_ps = pack.tile([P // LANES, LANES * K], F32)
        nc.tensor.matmul(packed_ps[:], of_group[:], blocks[:].rearrange("p s k -> p (s k)"), start=True, stop=True)
        packed = held.tile([P // LANES, LANES * K], F32)
        nc.vector.tensor_add(packed[:], packed_ps[:], third_one[:].rearrange("q s k -> q (s k)"))
        nc.sync.dma_start(out.rearrange("(q s) k -> q (s k)", s=LANES), packed[:])
